import numpy as np
import ml_dtypes


def mxq(x, axis, fmt="e4m3"):
    dtype, down = {"e4m3": (ml_dtypes.float8_e4m3fn, 7), "e5m2": (ml_dtypes.float8_e5m2, 14)}[fmt]
    v = np.moveaxis(np.asarray(x, np.float32).astype(ml_dtypes.bfloat16).astype(np.float64), axis, -1)
    blocks = v.reshape(v.shape[:-1] + (-1, 32))
    amax = np.abs(blocks).max(-1, keepdims=True)
    byte = np.maximum(np.where(amax > 0, np.frexp(amax)[1] - 1 + 127, 0) - down, 1)
    scale = np.exp2(byte - 127.0)
    codes = (blocks / scale).astype(np.float32).astype(dtype).astype(np.float64)
    return np.moveaxis((codes * scale).reshape(v.shape), -1, axis)


WIDE = False


def mx_kscale(k):
    if not WIDE:
        return np.ones(k)
    levels = np.array([10, -10, 5, -5, 0])
    a = np.random.permutation(np.resize(levels, k // 512 * 4)).reshape(k // 512, 4)
    idx = np.arange(k)
    return np.exp2(a[idx // 512, idx % 128 // 32])


BF16 = ml_dtypes.bfloat16


def bf(x):
    return np.asarray(x, np.float32).astype(BF16)


def f64(x):
    return np.asarray(x).astype(np.float64)


E2M1 = np.array([0.0, 0.5, 1.0, 1.5, 2.0, 3.0, 4.0, 6.0, -0.0, -0.5, -1.0, -1.5, -2.0, -3.0, -4.0, -6.0])


def pack_weight(w, fmt):
    k, n = w.shape
    w = f64(bf(w)).reshape(k // 32, 32, n)
    amax = np.abs(w).max(1)
    if fmt == "e4m3":
        byte = np.frexp(amax)[1] - 1 + 127 - 7
    else:
        mant, ex = np.frexp(amax / 6.0)
        byte = np.where(mant > 0.5, ex, ex - 1) + 127
    byte = np.clip(np.where(amax > 0, byte, 1), 1, 254)
    scaled = (w * np.exp2(127.0 - byte)[:, None, :]).reshape(k, n).astype(np.float32)
    by_word = np.ascontiguousarray(scaled.reshape(k // 512, 128, 4, n).transpose(0, 1, 3, 2))
    if fmt == "e4m3":
        words = by_word.astype(ml_dtypes.float8_e4m3fn).view(np.uint8)
    else:
        c = by_word.astype(ml_dtypes.float4_e2m1fn).view(np.uint8) & 0xF
        words = c[..., 0::2] | (c[..., 1::2] << 4)
    return np.ascontiguousarray(words), np.ascontiguousarray(byte.astype(np.uint8).reshape(k // 512, 16, n))


def unpack_weight(words, scales, fmt):
    g, p, n, _ = words.shape
    if fmt == "e4m3":
        vals = np.ascontiguousarray(words).view(ml_dtypes.float8_e4m3fn).astype(np.float64)
    else:
        nib = np.empty((g, p, n, 4), np.uint8)
        nib[..., 0::2] = words & 0xF
        nib[..., 1::2] = words >> 4
        vals = E2M1[nib]
    vals = vals * np.repeat(np.exp2(scales.astype(np.float64) - 127.0), 8, axis=1)[..., None]
    return vals.transpose(0, 1, 3, 2).reshape(g * 512, n)

def pack4(w):
    words, scales = pack_weight(w, "e2m1")
    return words.reshape(words.shape[0], 128, -1), scales


def unpack4(words, scales):
    return unpack_weight(words.reshape(words.shape[0], 128, -1, 2), scales, "e2m1")


B, D, H = 1024, 512, 1024


def sigmoid(v):
    return 1.0 / (1.0 + np.exp(-v))


def setup_inputs():
    s = mx_kscale(D)
    x = bf(np.random.standard_normal((B, D)) * s)
    w = np.random.standard_normal((4 * H, D)) * 1.5 / np.sqrt(D) / s[None, :]
    words, scales = pack4(np.ascontiguousarray(w.T))
    b_ih0 = bf(np.random.standard_normal(4 * H) * 0.3)
    b_hh0 = bf(np.random.standard_normal(4 * H) * 0.3)
    return {"x": x,
            "W_ih0_words": words,
            "W_ih0_scales": scales,
            "b_ih0": b_ih0,
            "b_hh0": b_hh0}


def reference(x, W_ih0_words, W_ih0_scales, b_ih0, b_hh0):
    wt = unpack4(W_ih0_words, W_ih0_scales)
    b = f64(b_ih0) + f64(b_hh0)
    xq = mxq(f64(x), 1, "e4m3")
    a_i = (xq @ wt[:, :H]) + b[:H]
    a_go = (xq @ wt[:, 2 * H:]) + b[2 * H:]
    a_g, a_o = a_go[:, :H], a_go[:, H:]
    c = sigmoid(a_i) * np.tanh(a_g)
    return sigmoid(a_o) * np.tanh(c)

@@ -1,0 +1,178 @@
+from contextlib import ExitStack
+
+import concourse.mybir as mybir
+from concourse.masks import make_identity
+
+F32 = mybir.dt.float32
+BF16 = mybir.dt.bfloat16
+I32 = mybir.dt.int32
+U32 = mybir.dt.uint32
+U8 = mybir.dt.uint8
+FP8X4 = mybir.dt.float8_e4m3fn_x4
+FP4X4 = mybir.dt.float4_e2m1fn_x4
+SIGMOID = mybir.ActivationFunctionType.Sigmoid
+TANH = mybir.ActivationFunctionType.Tanh
+ADD = mybir.AluOpType.add
+MULT = mybir.AluOpType.mult
+
+P = 128
+B = 1024
+K = 512
+H = 1024
+PACK = 4
+
+ROWS_PER_PARTITION = B // P
+CHUNK = 512
+BLOCKS = CHUNK // P
+PIECE = 256
+FIRST_PIECES = CHUNK // PIECE
+HIDDEN_TILES = H // P
+UNITS = (B // CHUNK) * HIDDEN_TILES
+
+GATES = (("i", 0, SIGMOID), ("g", 2, TANH), ("o", 3, SIGMOID))
+
+FLOPS = 2 * B * K * len(GATES) * H
+BYTES = (
+    B * K * 2
+    + len(GATES) * H * (K // 2 + K // 32)
+    + 2 * len(GATES) * H * 2
+    + B * H * 4
+)
+
+
+def tile_lstmbaseline_pa_kernel(tc, x, W_ih0_words, W_ih0_scales, b_ih0, b_hh0, out):
+    nc = tc.nc
+    x_rows = x.rearrange("(p t) k -> p t k", t=ROWS_PER_PARTITION)
+    out_rows = out.rearrange("(p t) n -> p t n", t=ROWS_PER_PARTITION)
+
+    with ExitStack() as stack:
+        keep = stack.enter_context(tc.tile_pool(name="keep", bufs=1))
+        work = stack.enter_context(tc.tile_pool(name="work", bufs=3))
+        sums = stack.enter_context(tc.psum_pool(name="sums", bufs=4))
+        turned = stack.enter_context(tc.psum_pool(name="turned", bufs=4))
+        stack.enter_context(tc.manual_schedule())
+
+        x_sb = keep.tile([P, ROWS_PER_PARTITION, K], BF16)
+        w_words = keep.tile([P, 2 * 4 * H], U8, align_bytes=64)
+        w_scales = keep.tile([P, 4 * H], U8, align_bytes=64)
+        b_ih_rows = keep.tile([32, P], BF16)
+        b_hh_rows = keep.tile([32, P], BF16)
+
+        def load_x_piece(q):
+            rows = slice(q * PIECE // P, (q + 1) * PIECE // P)
+            nc.sync.dma_start(out=x_sb[:, rows, :], in_=x_rows[:, rows, :])
+
+        nc.scalar.dma_start(out=b_ih_rows[:], in_=b_ih0.rearrange("(r c) -> r c", c=P))
+        nc.scalar.dma_start(out=b_hh_rows[:], in_=b_hh0.rearrange("(r c) -> r c", c=P))
+        load_x_piece(0)
+        load_x_piece(1)
+        nc.vector.memset(w_scales[:].bitcast(I32), 0)
+        for quadrant in range(4):
+            nc.sync.dma_start(
+                out=w_scales[32 * quadrant : 32 * quadrant + 4, :].bitcast(I32),
+                in_=W_ih0_scales[0, 4 * quadrant : 4 * quadrant + 4, :].bitcast(I32),
+            )
+        for name, position, func in GATES:
+            gate_bytes = slice(2 * H * position, 2 * H * (position + 1))
+            nc.sync.dma_start(
+                out=w_words[:, gate_bytes].bitcast(I32),
+                in_=W_ih0_words[0, :, gate_bytes].bitcast(I32),
+            )
+        load_x_piece(2)
+        load_x_piece(3)
+
+        identity = keep.tile([P, P], F32)
+        make_identity(nc, identity[:])
+
+        bias_rows = keep.tile([P, P], F32)
+        nc.vector.memset(bias_rows[:], 0.0)
+        nc.vector.tensor_tensor(out=bias_rows[0:32, :], in0=b_ih_rows[:], in1=b_hh_rows[:], op=ADD)
+        bias_turned = turned.tile([P, P], F32, tag="turned")
+        nc.tensor.transpose(bias_turned[:], bias_rows[:], identity[:])
+        bias = keep.tile([P, 32], F32)
+        nc.vector.tensor_copy(out=bias[:], in_=bias_turned[:, 0:32])
+
+        x_grouped = keep.tile([P, B, PACK], BF16, align_bytes=64)
+        x_codes = keep.tile([P, B], U32, align_bytes=64)
+        x_scales = keep.tile([P, B], U8, align_bytes=64)
+        x_pairs = x_sb[:].bitcast(F32)
+
+        def quantise_x_piece(q):
+            pairs_turned = turned.tile([P, PIECE // P, 2, P], F32, tag="turned")
+            for s in range(PIECE // P):
+                for u in range(2):
+                    nc.tensor.transpose(
+                        pairs_turned[:, s, u, :],
+                        x_pairs[:, q * PIECE // P + s, u : K // 2 : 2],
+                        identity[:],
+                    )
+            cols = slice(q * PIECE, (q + 1) * PIECE)
+            nc.vector.tensor_copy(
+                out=x_grouped[:, cols, :].bitcast(F32).rearrange("p (s b) u -> p s b u", b=P),
+                in_=pairs_turned[:].rearrange("p s u b -> p s b u"),
+            )
+            nc.vector.quantize_mx(
+                out=x_codes[:, cols].bitcast(FP8X4),
+                scales=x_scales[:, cols],
+                in_=x_grouped[:, cols, :].rearrange("p b t -> p (b t)"),
+            )
+
+        def gates(unit):
+            chunk, hidden_tile = divmod(unit, HIDDEN_TILES)
+            rows = slice(chunk * CHUNK, (chunk + 1) * CHUNK)
+            done = {}
+            for name, position, func in GATES:
+                n0 = position * H + hidden_tile * P
+                gate_sum = sums.tile([P, CHUNK], F32, tag="sum", name="sum_" + name)
+                nc.tensor.matmul_mx(
+                    out=gate_sum[:],
+                    lhsT=w_words[:, 2 * n0 : 2 * (n0 + P)].bitcast(FP4X4),
+                    lhsT_scale=w_scales[:, n0 : n0 + P],
+                    rhs=x_codes[:, rows].bitcast(FP8X4),
+                    rhs_scale=x_scales[:, rows],
+                    start=True,
+                    stop=True,
+                )
+                done[name] = work.tile([P, CHUNK], F32, name="gate_" + name)
+                nc.scalar.activation(
+                    out=done[name][:],
+                    in_=gate_sum[:],
+                    func=func,
+                    bias=bias[:, n0 // P : n0 // P + 1],
+                )
+            cell = work.tile([P, CHUNK], F32)
+            nc.vector.tensor_tensor(out=cell[:], in0=done["i"][:], in1=done["g"][:], op=MULT)
+            return cell, done["o"]
+
+        def turn_round(values, name):
+            flipped = turned.tile([P, BLOCKS, P], F32, tag="turned", name=name)
+            for s in range(BLOCKS):
+                nc.tensor.transpose(flipped[:, s, :], values[:, s * P : (s + 1) * P], identity[:])
+            return flipped
+
+        def finish(unit, cell, gate_o):
+            chunk, hidden_tile = divmod(unit, HIDDEN_TILES)
+            cell_turned = turn_round(cell, "cell_turned")
+            o_turned = turn_round(gate_o, "o_turned")
+            tanh_cell = work.tile([P, BLOCKS, P], F32)
+            nc.scalar.activation(out=tanh_cell[:], in_=cell_turned[:], func=TANH)
+            hidden = work.tile([P, BLOCKS, P], F32)
+            nc.vector.tensor_tensor(out=hidden[:], in0=tanh_cell[:], in1=o_turned[:], op=MULT)
+            nc.sync.dma_start(
+                out=out_rows[
+                    :, chunk * BLOCKS : (chunk + 1) * BLOCKS, hidden_tile * P : (hidden_tile + 1) * P
+                ],
+                in_=hidden[:],
+            )
+
+        for q in range(FIRST_PIECES):
+            quantise_x_piece(q)
+        waiting = None
+        for unit in range(UNITS):
+            started = gates(unit)
+            if unit < FIRST_PIECES:
+                quantise_x_piece(FIRST_PIECES + unit)
+            if waiting is not None:
+                finish(unit - 1, *waiting)
+            waiting = started
+        finish(UNITS - 1, *waiting)

@@ -62,8 +62,8 @@ def tile_lstmbaseline_pa_kernel(tc, x, W_ih0_words, W_ih0_scales, b_ih0, b_hh0, 
             rows = slice(q * PIECE // P, (q + 1) * PIECE // P)
             nc.sync.dma_start(out=x_sb[:, rows, :], in_=x_rows[:, rows, :])
 
-        nc.scalar.dma_start(out=b_ih_rows[:], in_=b_ih0.rearrange("(r c) -> r c", c=P))
-        nc.scalar.dma_start(out=b_hh_rows[:], in_=b_hh0.rearrange("(r c) -> r c", c=P))
+        nc.gpsimd.dma_start(out=b_ih_rows[:], in_=b_ih0.rearrange("(r c) -> r c", c=P))
+        nc.gpsimd.dma_start(out=b_hh_rows[:], in_=b_hh0.rearrange("(r c) -> r c", c=P))
         load_x_piece(0)
         load_x_piece(1)
         nc.vector.memset(w_scales[:].bitcast(I32), 0)
@@ -85,12 +85,14 @@ def tile_lstmbaseline_pa_kernel(tc, x, W_ih0_words, W_ih0_scales, b_ih0, b_hh0, 
         make_identity(nc, identity[:])
 
         bias_rows = keep.tile([P, P], F32)
-        nc.vector.memset(bias_rows[:], 0.0)
-        nc.vector.tensor_tensor(out=bias_rows[0:32, :], in0=b_ih_rows[:], in1=b_hh_rows[:], op=ADD)
-        bias_turned = turned.tile([P, P], F32, tag="turned")
-        nc.tensor.transpose(bias_turned[:], bias_rows[:], identity[:])
         bias = keep.tile([P, 32], F32)
-        nc.vector.tensor_copy(out=bias[:], in_=bias_turned[:, 0:32])
+        nc.gpsimd.memset(bias_rows[:], 0.0)
+        nc.gpsimd.tensor_tensor(out=bias_rows[0:32, :], in0=b_ih_rows[:], in1=b_hh_rows[:], op=ADD)
+
+        def turn_bias():
+            bias_turned = turned.tile([P, P], F32, tag="turned")
+            nc.tensor.transpose(bias_turned[:], bias_rows[:], identity[:])
+            nc.vector.tensor_copy(out=bias[:], in_=bias_turned[:, 0:32])
 
         x_grouped = keep.tile([P, B, PACK], BF16, align_bytes=64)
         x_codes = keep.tile([P, B], U32, align_bytes=64)
@@ -167,6 +169,7 @@ def tile_lstmbaseline_pa_kernel(tc, x, W_ih0_words, W_ih0_scales, b_ih0, b_hh0, 
 
         for q in range(FIRST_PIECES):
             quantise_x_piece(q)
+        turn_bias()
         waiting = None
         for unit in range(UNITS):
             started = gates(unit)

@@ -62,8 +62,8 @@ def tile_lstmbaseline_pa_kernel(tc, x, W_ih0_words, W_ih0_scales, b_ih0, b_hh0, 
             rows = slice(q * PIECE // P, (q + 1) * PIECE // P)
             nc.sync.dma_start(out=x_sb[:, rows, :], in_=x_rows[:, rows, :])
 
-        nc.gpsimd.dma_start(out=b_ih_rows[:], in_=b_ih0.rearrange("(r c) -> r c", c=P))
-        nc.gpsimd.dma_start(out=b_hh_rows[:], in_=b_hh0.rearrange("(r c) -> r c", c=P))
+        nc.scalar.dma_start(out=b_ih_rows[:], in_=b_ih0.rearrange("(r c) -> r c", c=P))
+        nc.scalar.dma_start(out=b_hh_rows[:], in_=b_hh0.rearrange("(r c) -> r c", c=P))
         load_x_piece(0)
         load_x_piece(1)
         nc.vector.memset(w_scales[:].bitcast(I32), 0)

@@ -23,11 +23,11 @@ PACK = 4
 
 ROWS_PER_PARTITION = B // P
 CHUNK = 512
-BLOCKS = CHUNK // P
-PIECE = 256
-FIRST_PIECES = CHUNK // PIECE
+EARLY_TILES = 3
 HIDDEN_TILES = H // P
-UNITS = (B // CHUNK) * HIDDEN_TILES
+LAG = 2
+WARM_UP_COLUMNS = 256
+WARM_UP_MATMULS = 9
 
 GATES = (("i", 0, SIGMOID), ("g", 2, TANH), ("o", 3, SIGMOID))
 
@@ -47,135 +47,183 @@ def tile_lstmbaseline_pa_kernel(tc, x, W_ih0_words, W_ih0_scales, b_ih0, b_hh0, 
 
     with ExitStack() as stack:
         keep = stack.enter_context(tc.tile_pool(name="keep", bufs=1))
-        work = stack.enter_context(tc.tile_pool(name="work", bufs=3))
-        sums = stack.enter_context(tc.psum_pool(name="sums", bufs=4))
-        turned = stack.enter_context(tc.psum_pool(name="turned", bufs=4))
+        work = stack.enter_context(tc.tile_pool(name="work", bufs=LAG + 2))
+        banks = stack.enter_context(tc.psum_pool(name="banks", bufs=8))
         stack.enter_context(tc.manual_schedule())
 
         x_sb = keep.tile([P, ROWS_PER_PARTITION, K], BF16)
-        w_words = keep.tile([P, 2 * 4 * H], U8, align_bytes=64)
-        w_scales = keep.tile([P, 4 * H], U8, align_bytes=64)
-        b_ih_rows = keep.tile([32, P], BF16)
-        b_hh_rows = keep.tile([32, P], BF16)
+        words_early = keep.tile([P, 4, EARLY_TILES * 2 * P], U8, align_bytes=64)
+        words_late = keep.tile([P, 4, (HIDDEN_TILES - EARLY_TILES) * 2 * P], U8, align_bytes=64)
+        scales_early = keep.tile([P, 4, EARLY_TILES * P], U8, align_bytes=64)
+        scales_late = keep.tile([P, 4, (HIDDEN_TILES - EARLY_TILES) * P], U8, align_bytes=64)
+        bias_rows = keep.tile([P, P], BF16)
+        words_hbm = W_ih0_words[0, :, :].bitcast(I32).rearrange("p (g c) -> p g c", g=4)
+        scales_hbm = W_ih0_scales[0, :, :].bitcast(I32).rearrange("r (g c) -> r g c", g=4)
+        early_words = EARLY_TILES * 2 * P // 4
+        early_scales = EARLY_TILES * P // 4
 
-        def load_x_piece(q):
-            rows = slice(q * PIECE // P, (q + 1) * PIECE // P)
-            nc.sync.dma_start(out=x_sb[:, rows, :], in_=x_rows[:, rows, :])
+        def load_x(engine, slot0, slot1):
+            engine.dma_start(out=x_sb[:, slot0:slot1, :], in_=x_rows[:, slot0:slot1, :])
 
-        nc.scalar.dma_start(out=b_ih_rows[:], in_=b_ih0.rearrange("(r c) -> r c", c=P))
-        nc.scalar.dma_start(out=b_hh_rows[:], in_=b_hh0.rearrange("(r c) -> r c", c=P))
-        load_x_piece(0)
-        load_x_piece(1)
-        nc.vector.memset(w_scales[:].bitcast(I32), 0)
-        for quadrant in range(4):
-            nc.sync.dma_start(
-                out=w_scales[32 * quadrant : 32 * quadrant + 4, :].bitcast(I32),
-                in_=W_ih0_scales[0, 4 * quadrant : 4 * quadrant + 4, :].bitcast(I32),
-            )
-        for name, position, func in GATES:
-            gate_bytes = slice(2 * H * position, 2 * H * (position + 1))
-            nc.sync.dma_start(
-                out=w_words[:, gate_bytes].bitcast(I32),
-                in_=W_ih0_words[0, :, gate_bytes].bitcast(I32),
-            )
-        load_x_piece(2)
-        load_x_piece(3)
+        def load_scales(scales_tile, c0, c1):
+            nc.vector.memset(scales_tile[:].bitcast(I32), 0)
+            for quadrant in range(4):
+                nc.sync.dma_start(
+                    out=scales_tile[32 * quadrant : 32 * quadrant + 4, :, :].bitcast(I32),
+                    in_=scales_hbm[4 * quadrant : 4 * quadrant + 4, :, c0:c1],
+                )
+
+        zeros_words = keep.tile([P, WARM_UP_COLUMNS // 2], F32)
+        nc.vector.memset(zeros_words[:], 0.0)
+        zeros = zeros_words[:].bitcast(BF16)
+
+        warm_in = keep.tile([P, 1], F32)
+        warm_out = keep.tile([P, 1], F32)
+        nc.vector.memset(warm_in[:], 0.0)
+        nc.scalar.activation(out=warm_out[:], in_=warm_in[:], func=SIGMOID)
+
+        load_x(nc.sync, 0, 2)
+        load_x(nc.gpsimd, 2, 4)
+        nc.sync.dma_start(out=bias_rows[0:32, :], in_=b_ih0.rearrange("(r c) -> r c", c=P))
+        nc.sync.dma_start(out=bias_rows[32:64, :], in_=b_hh0.rearrange("(r c) -> r c", c=P))
+        nc.sync.dma_start(out=words_early[:].bitcast(I32), in_=words_hbm[:, :, 0:early_words])
+        load_scales(scales_early, 0, early_scales)
+        load_scales(scales_late, early_scales, H // 4)
+        nc.sync.dma_start(out=words_late[:, 0, :].bitcast(I32), in_=words_hbm[:, 0, early_words:])
+        nc.sync.dma_start(out=words_late[:, 2:4, :].bitcast(I32), in_=words_hbm[:, 2:4, early_words:])
+        load_x(nc.sync, 4, 8)
+
+        idle_sum = banks.tile([P, WARM_UP_COLUMNS], F32, tag="bank")
+        for repeat in range(WARM_UP_MATMULS):
+            nc.tensor.matmul(idle_sum[:], lhsT=zeros[:, 0:P], rhs=zeros, start=True, stop=True)
 
         identity = keep.tile([P, P], F32)
         make_identity(nc, identity[:])
 
-        bias_rows = keep.tile([P, P], F32)
+        pick = keep.tile([P, 32], BF16)
         bias = keep.tile([P, 32], F32)
-        nc.gpsimd.memset(bias_rows[:], 0.0)
-        nc.gpsimd.tensor_tensor(out=bias_rows[0:32, :], in0=b_ih_rows[:], in1=b_hh_rows[:], op=ADD)
-
-        def turn_bias():
-            bias_turned = turned.tile([P, P], F32, tag="turned")
-            nc.tensor.transpose(bias_turned[:], bias_rows[:], identity[:])
-            nc.vector.tensor_copy(out=bias[:], in_=bias_turned[:, 0:32])
+        nc.vector.memset(bias_rows[64:128, :], 0.0)
+        nc.vector.tensor_tensor(out=pick[:], in0=identity[:, 0:32], in1=identity[:, 32:64], op=ADD)
 
         x_grouped = keep.tile([P, B, PACK], BF16, align_bytes=64)
         x_codes = keep.tile([P, B], U32, align_bytes=64)
         x_scales = keep.tile([P, B], U8, align_bytes=64)
         x_pairs = x_sb[:].bitcast(F32)
 
-        def quantise_x_piece(q):
-            pairs_turned = turned.tile([P, PIECE // P, 2, P], F32, tag="turned")
-            for s in range(PIECE // P):
+        def turn_x(slot0, slots):
+            pairs_turned = banks.tile([P, slots, 2, P], F32, tag="bank")
+            for s in range(slots):
                 for u in range(2):
                     nc.tensor.transpose(
-                        pairs_turned[:, s, u, :],
-                        x_pairs[:, q * PIECE // P + s, u : K // 2 : 2],
-                        identity[:],
+                        pairs_turned[:, s, u, :], x_pairs[:, slot0 + s, u : K // 2 : 2], identity[:]
                     )
-            cols = slice(q * PIECE, (q + 1) * PIECE)
-            nc.vector.tensor_copy(
+            return pairs_turned
+
+        def group_x(copy, slot0, slots, pairs_turned):
+            cols = slice(slot0 * P, (slot0 + slots) * P)
+            copy(
                 out=x_grouped[:, cols, :].bitcast(F32).rearrange("p (s b) u -> p s b u", b=P),
                 in_=pairs_turned[:].rearrange("p s u b -> p s b u"),
             )
+
+        def quantise_x(slot0, slots):
+            cols = slice(slot0 * P, (slot0 + slots) * P)
             nc.vector.quantize_mx(
                 out=x_codes[:, cols].bitcast(FP8X4),
                 scales=x_scales[:, cols],
                 in_=x_grouped[:, cols, :].rearrange("p b t -> p (b t)"),
             )
 
-        def gates(unit):
-            chunk, hidden_tile = divmod(unit, HIDDEN_TILES)
-            rows = slice(chunk * CHUNK, (chunk + 1) * CHUNK)
-            done = {}
+        def matmuls(unit):
+            hidden_tile, col0, cols = unit
+            if hidden_tile < EARLY_TILES:
+                words, scales, n0 = words_early, scales_early, hidden_tile * P
+            else:
+                words, scales, n0 = words_late, scales_late, (hidden_tile - EARLY_TILES) * P
+            gate_sums = {}
             for name, position, func in GATES:
-                n0 = position * H + hidden_tile * P
-                gate_sum = sums.tile([P, CHUNK], F32, tag="sum", name="sum_" + name)
+                gate_sums[name] = banks.tile([P, cols], F32, tag="bank", name="sum_" + name)
                 nc.tensor.matmul_mx(
-                    out=gate_sum[:],
-                    lhsT=w_words[:, 2 * n0 : 2 * (n0 + P)].bitcast(FP4X4),
-                    lhsT_scale=w_scales[:, n0 : n0 + P],
-                    rhs=x_codes[:, rows].bitcast(FP8X4),
-                    rhs_scale=x_scales[:, rows],
+                    out=gate_sums[name][:],
+                    lhsT=words[:, position, 2 * n0 : 2 * (n0 + P)].bitcast(FP4X4),
+                    lhsT_scale=scales[:, position, n0 : n0 + P],
+                    rhs=x_codes[:, col0 : col0 + cols].bitcast(FP8X4),
+                    rhs_scale=x_scales[:, col0 : col0 + cols],
                     start=True,
                     stop=True,
                 )
-                done[name] = work.tile([P, CHUNK], F32, name="gate_" + name)
+            return gate_sums
+
+        def activations(unit, gate_sums):
+            hidden_tile, col0, cols = unit
+            done = {}
+            for name, position, func in GATES:
+                bias_column = position * HIDDEN_TILES + hidden_tile
+                done[name] = work.tile([P, cols], F32, name="gate_" + name)
                 nc.scalar.activation(
                     out=done[name][:],
-                    in_=gate_sum[:],
+                    in_=gate_sums[name][:],
                     func=func,
-                    bias=bias[:, n0 // P : n0 // P + 1],
+                    bias=bias[:, bias_column : bias_column + 1],
                 )
-            cell = work.tile([P, CHUNK], F32)
+            cell = work.tile([P, cols], F32)
             nc.vector.tensor_tensor(out=cell[:], in0=done["i"][:], in1=done["g"][:], op=MULT)
             return cell, done["o"]
 
-        def turn_round(values, name):
-            flipped = turned.tile([P, BLOCKS, P], F32, tag="turned", name=name)
-            for s in range(BLOCKS):
+        def turn_round(values, blocks, name):
+            flipped = banks.tile([P, blocks, P], F32, tag="bank", name=name)
+            for s in range(blocks):
                 nc.tensor.transpose(flipped[:, s, :], values[:, s * P : (s + 1) * P], identity[:])
             return flipped
 
         def finish(unit, cell, gate_o):
-            chunk, hidden_tile = divmod(unit, HIDDEN_TILES)
-            cell_turned = turn_round(cell, "cell_turned")
-            o_turned = turn_round(gate_o, "o_turned")
-            tanh_cell = work.tile([P, BLOCKS, P], F32)
+            hidden_tile, col0, cols = unit
+            blocks = cols // P
+            cell_turned = turn_round(cell, blocks, "cell_turned")
+            o_turned = turn_round(gate_o, blocks, "o_turned")
+            tanh_cell = work.tile([P, blocks, P], F32)
             nc.scalar.activation(out=tanh_cell[:], in_=cell_turned[:], func=TANH)
-            hidden = work.tile([P, BLOCKS, P], F32)
+            hidden = work.tile([P, blocks, P], F32)
             nc.vector.tensor_tensor(out=hidden[:], in0=tanh_cell[:], in1=o_turned[:], op=MULT)
             nc.sync.dma_start(
                 out=out_rows[
-                    :, chunk * BLOCKS : (chunk + 1) * BLOCKS, hidden_tile * P : (hidden_tile + 1) * P
+                    :, col0 // P : col0 // P + blocks, hidden_tile * P : (hidden_tile + 1) * P
                 ],
                 in_=hidden[:],
             )
 
-        for q in range(FIRST_PIECES):
-            quantise_x_piece(q)
-        turn_bias()
-        waiting = None
-        for unit in range(UNITS):
-            started = gates(unit)
-            if unit < FIRST_PIECES:
-                quantise_x_piece(FIRST_PIECES + unit)
-            if waiting is not None:
-                finish(unit - 1, *waiting)
-            waiting = started
-        finish(UNITS - 1, *waiting)
+        units = [(0, 0, P), (0, P, P)]
+        units += [(hidden_tile, 0, CHUNK // 2) for hidden_tile in range(1, EARLY_TILES)]
+        units += [(hidden_tile, CHUNK // 2, CHUNK // 2) for hidden_tile in range(EARLY_TILES)]
+        units += [(hidden_tile, 0, CHUNK) for hidden_tile in range(EARLY_TILES, HIDDEN_TILES)]
+        units += [(hidden_tile, CHUNK, CHUNK) for hidden_tile in range(HIDDEN_TILES)]
+        later_x = {8: (4, 2), 9: (6, 2)}
+
+        first_turned = turn_x(0, 1)
+        second_turned = turn_x(1, 1)
+        bias_sum = banks.tile([P, 32], F32, tag="bank")
+        nc.tensor.matmul(bias_sum[:], lhsT=bias_rows[:], rhs=pick[:], start=True, stop=True)
+        group_x(nc.vector.tensor_copy, 0, 1, first_turned)
+        group_x(nc.scalar.copy, 1, 1, second_turned)
+        nc.vector.tensor_copy(out=bias[:], in_=bias_sum[:])
+        quantise_x(0, 1)
+        quantise_x(1, 1)
+
+        waiting = []
+        for index, unit in enumerate(units):
+            gate_sums = matmuls(unit)
+            if index == 2:
+                group_x(nc.vector.tensor_copy, 2, 2, turn_x(2, 2))
+                quantise_x(2, 2)
+            if index in later_x:
+                pairs_turned = turn_x(*later_x[index])
+            waiting.append((unit, activations(unit, gate_sums)))
+            if index in later_x:
+                group_x(nc.vector.tensor_copy, *later_x[index], pairs_turned)
+            if index - 1 in later_x:
+                quantise_x(*later_x[index - 1])
+            if len(waiting) > LAG:
+                finish(waiting[0][0], *waiting[0][1])
+                waiting = waiting[1:]
+        for unit, started in waiting:
+            finish(unit, *started)

@@ -196,7 +196,8 @@ def tile_lstmbaseline_pa_kernel(tc, x, W_ih0_words, W_ih0_scales, b_ih0, b_hh0, 
         units += [(hidden_tile, 0, CHUNK // 2) for hidden_tile in range(1, EARLY_TILES)]
         units += [(hidden_tile, CHUNK // 2, CHUNK // 2) for hidden_tile in range(EARLY_TILES)]
         units += [(hidden_tile, 0, CHUNK) for hidden_tile in range(EARLY_TILES, HIDDEN_TILES)]
-        units += [(hidden_tile, CHUNK, CHUNK) for hidden_tile in range(HIDDEN_TILES)]
+        units += [(hidden_tile, CHUNK, CHUNK) for hidden_tile in range(HIDDEN_TILES - 1)]
+        units += [(HIDDEN_TILES - 1, col0, CHUNK // 2) for col0 in (CHUNK, CHUNK + CHUNK // 2)]
         later_x = {8: (4, 2), 9: (6, 2)}
 
         first_turned = turn_x(0, 1)

@@ -26,6 +26,18 @@ CHUNK = 512
 EARLY_TILES = 3
 HIDDEN_TILES = H // P
 LAG = 2
+TANH_LEAD = 0.00012132876240913503
+TANH_TAIL = (
+    8242.068738109192,
+    -2747.3558099211377,
+    1098.930339531672,
+    -444.67906624908534,
+    179.53518132355708,
+    -70.81795216358458,
+    25.354931336378282,
+    -6.924973475538237,
+)
+VECTOR_UNITS = (7,)
 WARM_UP_COLUMNS = 256
 WARM_UP_MATMULS = 9
 
@@ -49,6 +61,7 @@ def tile_lstmbaseline_pa_kernel(tc, x, W_ih0_words, W_ih0_scales, b_ih0, b_hh0, 
         keep = stack.enter_context(tc.tile_pool(name="keep", bufs=1))
         work = stack.enter_context(tc.tile_pool(name="work", bufs=LAG + 2))
         banks = stack.enter_context(tc.psum_pool(name="banks", bufs=8))
+        slow = stack.enter_context(tc.tile_pool(name="slow", bufs=2))
         stack.enter_context(tc.manual_schedule())
 
         x_sb = keep.tile([P, ROWS_PER_PARTITION, K], BF16)
@@ -154,19 +167,19 @@ def tile_lstmbaseline_pa_kernel(tc, x, W_ih0_words, W_ih0_scales, b_ih0, b_hh0, 
                 )
             return gate_sums
 
-        def activations(unit, gate_sums):
+        def activations(unit, gate_sums, pool):
             hidden_tile, col0, cols = unit
             done = {}
             for name, position, func in GATES:
                 bias_column = position * HIDDEN_TILES + hidden_tile
-                done[name] = work.tile([P, cols], F32, name="gate_" + name)
+                done[name] = pool.tile([P, cols], F32, name="gate_" + name)
                 nc.scalar.activation(
                     out=done[name][:],
                     in_=gate_sums[name][:],
                     func=func,
                     bias=bias[:, bias_column : bias_column + 1],
                 )
-            cell = work.tile([P, cols], F32)
+            cell = pool.tile([P, cols], F32, name="cell")
             nc.vector.tensor_tensor(out=cell[:], in0=done["i"][:], in1=done["g"][:], op=MULT)
             return cell, done["o"]
 
@@ -192,6 +205,47 @@ def tile_lstmbaseline_pa_kernel(tc, x, W_ih0_words, W_ih0_scales, b_ih0, b_hh0, 
                 in_=hidden[:],
             )
 
+        def finish_on_vector(unit, cell, gate_o):
+            hidden_tile, col0, cols = unit
+            blocks = cols // P
+            state = {}
+
+            def square():
+                state["u"] = slow.tile([P, cols], F32, name="c_squared")
+                state["t"] = state["u"]
+                nc.vector.tensor_tensor(out=state["u"][:], in0=cell[:], in1=cell[:], op=MULT)
+
+            def horner(coefficient, factor):
+                previous = state["t"]
+                state["t"] = slow.tile([P, cols], F32, name="horner")
+                nc.vector.scalar_tensor_tensor(
+                    out=state["t"][:], in0=previous[:], scalar=coefficient, in1=factor[:], op0=ADD, op1=MULT
+                )
+
+            def times_o():
+                state["h"] = slow.tile([P, cols], F32, name="hidden_unturned")
+                nc.vector.scalar_tensor_tensor(
+                    out=state["h"][:], in0=state["t"][:], scalar=TANH_LEAD, in1=gate_o[:], op0=MULT, op1=MULT
+                )
+
+            def turn():
+                state["turned"] = turn_round(state["h"], blocks, "hidden_turned")
+
+            def leave():
+                hidden = slow.tile([P, blocks, P], F32, name="hidden_by_vector")
+                nc.vector.tensor_copy(out=hidden[:], in_=state["turned"][:])
+                nc.sync.dma_start(
+                    out=out_rows[
+                        :, col0 // P : col0 // P + blocks, hidden_tile * P : (hidden_tile + 1) * P
+                    ],
+                    in_=hidden[:],
+                )
+
+            steps = [square]
+            steps += [lambda k=k: horner(TANH_TAIL[k], state["u"]) for k in range(7, 0, -1)]
+            steps += [lambda: horner(TANH_TAIL[0], cell), times_o, lambda: None, turn, leave]
+            return steps
+
         units = [(0, 0, P), (0, P, P)]
         units += [(hidden_tile, 0, CHUNK // 2) for hidden_tile in range(1, EARLY_TILES)]
         units += [(hidden_tile, CHUNK // 2, CHUNK // 2) for hidden_tile in range(EARLY_TILES)]
@@ -211,6 +265,7 @@ def tile_lstmbaseline_pa_kernel(tc, x, W_ih0_words, W_ih0_scales, b_ih0, b_hh0, 
         quantise_x(1, 1)
 
         waiting = []
+        vector_steps = []
         for index, unit in enumerate(units):
             gate_sums = matmuls(unit)
             if index == 2:
@@ -218,7 +273,10 @@ def tile_lstmbaseline_pa_kernel(tc, x, W_ih0_words, W_ih0_scales, b_ih0, b_hh0, 
                 quantise_x(2, 2)
             if index in later_x:
                 pairs_turned = turn_x(*later_x[index])
-            waiting.append((unit, activations(unit, gate_sums)))
+            if index in VECTOR_UNITS:
+                vector_steps += finish_on_vector(unit, *activations(unit, gate_sums, slow))
+            else:
+                waiting.append((unit, activations(unit, gate_sums, work)))
             if index in later_x:
                 group_x(nc.vector.tensor_copy, *later_x[index], pairs_turned)
             if index - 1 in later_x:
@@ -226,5 +284,10 @@ def tile_lstmbaseline_pa_kernel(tc, x, W_ih0_words, W_ih0_scales, b_ih0, b_hh0, 
             if len(waiting) > LAG:
                 finish(waiting[0][0], *waiting[0][1])
                 waiting = waiting[1:]
+            if vector_steps:
+                vector_steps[0]()
+                vector_steps = vector_steps[1:]
+        for step in vector_steps:
+            step()
         for unit, started in waiting:
             finish(unit, *started)

@@ -96,11 +96,11 @@ def tile_lstmbaseline_pa_kernel(tc, x, W_ih0_words, W_ih0_scales, b_ih0, b_hh0, 
         nc.scalar.activation(out=warm_out[:], in_=warm_in[:], func=SIGMOID)
 
         load_x(nc.sync, 0, 2)
-        load_x(nc.gpsimd, 2, 4)
         nc.sync.dma_start(out=bias_rows[0:32, :], in_=b_ih0.rearrange("(r c) -> r c", c=P))
         nc.sync.dma_start(out=bias_rows[32:64, :], in_=b_hh0.rearrange("(r c) -> r c", c=P))
         nc.sync.dma_start(out=words_early[:].bitcast(I32), in_=words_hbm[:, :, 0:early_words])
         load_scales(scales_early, 0, early_scales)
+        load_x(nc.sync, 2, 4)
         load_scales(scales_late, early_scales, H // 4)
         nc.sync.dma_start(out=words_late[:, 0, :].bitcast(I32), in_=words_hbm[:, 0, early_words:])
         nc.sync.dma_start(out=words_late[:, 2:4, :].bitcast(I32), in_=words_hbm[:, 2:4, early_words:])

@@ -37,7 +37,7 @@ TANH_TAIL = (
     25.354931336378282,
     -6.924973475538237,
 )
-VECTOR_UNITS = (7,)
+VECTOR_BLOCKS = (1,)
 WARM_UP_COLUMNS = 256
 WARM_UP_MATMULS = 9
 
@@ -95,12 +95,11 @@ def tile_lstmbaseline_pa_kernel(tc, x, W_ih0_words, W_ih0_scales, b_ih0, b_hh0, 
         nc.vector.memset(warm_in[:], 0.0)
         nc.scalar.activation(out=warm_out[:], in_=warm_in[:], func=SIGMOID)
 
-        load_x(nc.sync, 0, 2)
+        load_x(nc.sync, 0, 4)
         nc.sync.dma_start(out=bias_rows[0:32, :], in_=b_ih0.rearrange("(r c) -> r c", c=P))
         nc.sync.dma_start(out=bias_rows[32:64, :], in_=b_hh0.rearrange("(r c) -> r c", c=P))
         nc.sync.dma_start(out=words_early[:].bitcast(I32), in_=words_hbm[:, :, 0:early_words])
         load_scales(scales_early, 0, early_scales)
-        load_x(nc.sync, 2, 4)
         load_scales(scales_late, early_scales, H // 4)
         nc.sync.dma_start(out=words_late[:, 0, :].bitcast(I32), in_=words_hbm[:, 0, early_words:])
         nc.sync.dma_start(out=words_late[:, 2:4, :].bitcast(I32), in_=words_hbm[:, 2:4, early_words:])
@@ -167,21 +166,23 @@ def tile_lstmbaseline_pa_kernel(tc, x, W_ih0_words, W_ih0_scales, b_ih0, b_hh0, 
                 )
             return gate_sums
 
-        def activations(unit, gate_sums, pool):
+        def activations(unit, gate_sums, pool, cell, gate_o, offset):
             hidden_tile, col0, cols = unit
-            done = {}
+            done = {"o": gate_o[:, offset : offset + cols]}
+            for name in ("i", "g"):
+                gate_tile = pool.tile([P, cols], F32, name="gate_" + name)
+                done[name] = gate_tile[:]
             for name, position, func in GATES:
                 bias_column = position * HIDDEN_TILES + hidden_tile
-                done[name] = pool.tile([P, cols], F32, name="gate_" + name)
                 nc.scalar.activation(
-                    out=done[name][:],
+                    out=done[name],
                     in_=gate_sums[name][:],
                     func=func,
                     bias=bias[:, bias_column : bias_column + 1],
                 )
-            cell = pool.tile([P, cols], F32, name="cell")
-            nc.vector.tensor_tensor(out=cell[:], in0=done["i"][:], in1=done["g"][:], op=MULT)
-            return cell, done["o"]
+            nc.vector.tensor_tensor(
+                out=cell[:, offset : offset + cols], in0=done["i"], in1=done["g"], op=MULT
+            )
 
         def turn_round(values, blocks, name):
             flipped = banks.tile([P, blocks, P], F32, tag="bank", name=name)
@@ -246,48 +247,59 @@ def tile_lstmbaseline_pa_kernel(tc, x, W_ih0_words, W_ih0_scales, b_ih0, b_hh0, 
             steps += [lambda: horner(TANH_TAIL[0], cell), times_o, lambda: None, turn, leave]
             return steps
 
-        units = [(0, 0, P), (0, P, P)]
-        units += [(hidden_tile, 0, CHUNK // 2) for hidden_tile in range(1, EARLY_TILES)]
-        units += [(hidden_tile, CHUNK // 2, CHUNK // 2) for hidden_tile in range(EARLY_TILES)]
-        units += [(hidden_tile, 0, CHUNK) for hidden_tile in range(EARLY_TILES, HIDDEN_TILES)]
-        units += [(hidden_tile, CHUNK, CHUNK) for hidden_tile in range(HIDDEN_TILES - 1)]
-        units += [(HIDDEN_TILES - 1, col0, CHUNK // 2) for col0 in (CHUNK, CHUNK + CHUNK // 2)]
-        later_x = {8: (4, 2), 9: (6, 2)}
+        blocks = [(0, 0, CHUNK, (P, P, CHUNK // 2))]
+        blocks += [(hidden_tile, 0, CHUNK, (CHUNK,)) for hidden_tile in range(1, HIDDEN_TILES)]
+        blocks += [(hidden_tile, CHUNK, CHUNK, (CHUNK,)) for hidden_tile in range(HIDDEN_TILES - 1)]
+        blocks += [
+            (HIDDEN_TILES - 1, col0, CHUNK // 2, (CHUNK // 2,)) for col0 in (CHUNK, CHUNK + CHUNK // 2)
+        ]
+        later_x = {6: (4, 2), 7: (6, 2)}
 
         first_turned = turn_x(0, 1)
         second_turned = turn_x(1, 1)
         bias_sum = banks.tile([P, 32], F32, tag="bank")
         nc.tensor.matmul(bias_sum[:], lhsT=bias_rows[:], rhs=pick[:], start=True, stop=True)
+        third_turned = turn_x(2, 2)
         group_x(nc.vector.tensor_copy, 0, 1, first_turned)
         group_x(nc.scalar.copy, 1, 1, second_turned)
         nc.vector.tensor_copy(out=bias[:], in_=bias_sum[:])
         quantise_x(0, 1)
         quantise_x(1, 1)
+        group_x(nc.vector.tensor_copy, 2, 2, third_turned)
+        quantise_x(2, 2)
 
         waiting = []
         vector_steps = []
-        for index, unit in enumerate(units):
-            gate_sums = matmuls(unit)
-            if index == 2:
-                group_x(nc.vector.tensor_copy, 2, 2, turn_x(2, 2))
-                quantise_x(2, 2)
-            if index in later_x:
-                pairs_turned = turn_x(*later_x[index])
-            if index in VECTOR_UNITS:
-                vector_steps += finish_on_vector(unit, *activations(unit, gate_sums, slow))
-            else:
-                waiting.append((unit, activations(unit, gate_sums, work)))
-            if index in later_x:
-                group_x(nc.vector.tensor_copy, *later_x[index], pairs_turned)
-            if index - 1 in later_x:
-                quantise_x(*later_x[index - 1])
-            if len(waiting) > LAG:
-                finish(waiting[0][0], *waiting[0][1])
-                waiting = waiting[1:]
-            if vector_steps:
-                vector_steps[0]()
-                vector_steps = vector_steps[1:]
+        index = 0
+        for number, (hidden_tile, col0, cols, widths) in enumerate(blocks):
+            pool = slow if number in VECTOR_BLOCKS else work
+            cell = pool.tile([P, cols], F32, name="cell")
+            gate_o = pool.tile([P, cols], F32, name="gate_o")
+            offset = 0
+            for width in widths:
+                unit = (hidden_tile, col0 + offset, width)
+                gate_sums = matmuls(unit)
+                if index in later_x:
+                    pairs_turned = turn_x(*later_x[index])
+                activations(unit, gate_sums, pool, cell, gate_o, offset)
+                offset += width
+                if offset == cols:
+                    if number in VECTOR_BLOCKS:
+                        vector_steps += finish_on_vector((hidden_tile, col0, cols), cell, gate_o)
+                    else:
+                        waiting.append(((hidden_tile, col0, cols), cell, gate_o))
+                if index in later_x:
+                    group_x(nc.vector.tensor_copy, *later_x[index], pairs_turned)
+                if index - 1 in later_x:
+                    quantise_x(*later_x[index - 1])
+                if len(waiting) > LAG:
+                    finish(*waiting[0])
+                    waiting = waiting[1:]
+                if vector_steps:
+                    vector_steps[0]()
+                    vector_steps = vector_steps[1:]
+                index += 1
         for step in vector_steps:
             step()
-        for unit, started in waiting:
-            finish(unit, *started)
+        for block in waiting:
+            finish(*block)

@@ -90,16 +90,17 @@ def tile_lstmbaseline_pa_kernel(tc, x, W_ih0_words, W_ih0_scales, b_ih0, b_hh0, 
         nc.vector.memset(zeros_words[:], 0.0)
         zeros = zeros_words[:].bitcast(BF16)
 
+        load_x(nc.sync, 0, 4)
+        load_scales(scales_early, 0, early_scales)
+
         warm_in = keep.tile([P, 1], F32)
         warm_out = keep.tile([P, 1], F32)
         nc.vector.memset(warm_in[:], 0.0)
         nc.scalar.activation(out=warm_out[:], in_=warm_in[:], func=SIGMOID)
 
-        load_x(nc.sync, 0, 4)
         nc.sync.dma_start(out=bias_rows[0:32, :], in_=b_ih0.rearrange("(r c) -> r c", c=P))
         nc.sync.dma_start(out=bias_rows[32:64, :], in_=b_hh0.rearrange("(r c) -> r c", c=P))
         nc.sync.dma_start(out=words_early[:].bitcast(I32), in_=words_hbm[:, :, 0:early_words])
-        load_scales(scales_early, 0, early_scales)
         load_scales(scales_late, early_scales, H // 4)
         nc.sync.dma_start(out=words_late[:, 0, :].bitcast(I32), in_=words_hbm[:, 0, early_words:])
         nc.sync.dma_start(out=words_late[:, 2:4, :].bitcast(I32), in_=words_hbm[:, 2:4, early_words:])

@@ -37,7 +37,7 @@ TANH_TAIL = (
     25.354931336378282,
     -6.924973475538237,
 )
-VECTOR_BLOCKS = (1,)
+VECTOR_BLOCKS = (0, 1)
 WARM_UP_COLUMNS = 256
 WARM_UP_MATMULS = 9
 
@@ -213,13 +213,13 @@ def tile_lstmbaseline_pa_kernel(tc, x, W_ih0_words, W_ih0_scales, b_ih0, b_hh0, 
             state = {}
 
             def square():
-                state["u"] = slow.tile([P, cols], F32, name="c_squared")
+                state["u"] = slow.tile([P, cols], F32, name="c_squared_%d" % hidden_tile)
                 state["t"] = state["u"]
                 nc.vector.tensor_tensor(out=state["u"][:], in0=cell[:], in1=cell[:], op=MULT)
 
             def horner(coefficient, factor):
                 previous = state["t"]
-                state["t"] = slow.tile([P, cols], F32, name="horner")
+                state["t"] = slow.tile([P, cols], F32, name="horner_%d" % hidden_tile)
                 nc.vector.scalar_tensor_tensor(
                     out=state["t"][:], in0=previous[:], scalar=coefficient, in1=factor[:], op0=ADD, op1=MULT
                 )
@@ -269,8 +269,18 @@ def tile_lstmbaseline_pa_kernel(tc, x, W_ih0_words, W_ih0_scales, b_ih0, b_hh0, 
         group_x(nc.vector.tensor_copy, 2, 2, third_turned)
         quantise_x(2, 2)
 
+        def advance(pending, moved):
+            if pending:
+                chain = pending[0]
+                pending.remove(chain)
+                chain[0]()
+                chain.remove(chain[0])
+                if chain:
+                    moved.append(chain)
+
         waiting = []
-        vector_steps = []
+        pending = []
+        moved = []
         index = 0
         for number, (hidden_tile, col0, cols, widths) in enumerate(blocks):
             pool = slow if number in VECTOR_BLOCKS else work
@@ -284,23 +294,26 @@ def tile_lstmbaseline_pa_kernel(tc, x, W_ih0_words, W_ih0_scales, b_ih0, b_hh0, 
                     pairs_turned = turn_x(*later_x[index])
                 activations(unit, gate_sums, pool, cell, gate_o, offset)
                 offset += width
-                if offset == cols:
-                    if number in VECTOR_BLOCKS:
-                        vector_steps += finish_on_vector((hidden_tile, col0, cols), cell, gate_o)
-                    else:
-                        waiting.append(((hidden_tile, col0, cols), cell, gate_o))
                 if index in later_x:
                     group_x(nc.vector.tensor_copy, *later_x[index], pairs_turned)
                 if index - 1 in later_x:
                     quantise_x(*later_x[index - 1])
+                if index not in later_x and index - 1 not in later_x:
+                    advance(pending, moved)
+                if offset == cols:
+                    if number in VECTOR_BLOCKS:
+                        pending.append(finish_on_vector((hidden_tile, col0, cols), cell, gate_o))
+                    else:
+                        waiting.append(((hidden_tile, col0, cols), cell, gate_o))
                 if len(waiting) > LAG:
                     finish(*waiting[0])
                     waiting = waiting[1:]
-                if vector_steps:
-                    vector_steps[0]()
-                    vector_steps = vector_steps[1:]
+                advance(pending, moved)
+                pending.extend(moved)
+                moved.clear()
                 index += 1
-        for step in vector_steps:
-            step()
+        for chain in pending:
+            for step in chain:
+                step()
         for block in waiting:
             finish(*block)

@@ -37,7 +37,9 @@ TANH_TAIL = (
     25.354931336378282,
     -6.924973475538237,
 )
-VECTOR_BLOCKS = (0, 1)
+VECTOR_BLOCKS = (0, 3, 6, 9)
+STEPS_PER_UNIT = 6
+LAST_ON_VECTOR = 2
 WARM_UP_COLUMNS = 256
 WARM_UP_MATMULS = 9
 
@@ -60,8 +62,10 @@ def tile_lstmbaseline_pa_kernel(tc, x, W_ih0_words, W_ih0_scales, b_ih0, b_hh0, 
     with ExitStack() as stack:
         keep = stack.enter_context(tc.tile_pool(name="keep", bufs=1))
         work = stack.enter_context(tc.tile_pool(name="work", bufs=LAG + 2))
-        banks = stack.enter_context(tc.psum_pool(name="banks", bufs=8))
+        banks = stack.enter_context(tc.psum_pool(name="banks", bufs=7))
+        held = stack.enter_context(tc.psum_pool(name="held", bufs=1))
         slow = stack.enter_context(tc.tile_pool(name="slow", bufs=2))
+        leaving = stack.enter_context(tc.tile_pool(name="leaving", bufs=8))
         stack.enter_context(tc.manual_schedule())
 
         x_sb = keep.tile([P, ROWS_PER_PARTITION, K], BF16)
@@ -167,11 +171,11 @@ def tile_lstmbaseline_pa_kernel(tc, x, W_ih0_words, W_ih0_scales, b_ih0, b_hh0, 
                 )
             return gate_sums
 
-        def activations(unit, gate_sums, pool, cell, gate_o, offset):
+        def activations(unit, gate_sums, engine, cell, gate_o, offset):
             hidden_tile, col0, cols = unit
             done = {"o": gate_o[:, offset : offset + cols]}
             for name in ("i", "g"):
-                gate_tile = pool.tile([P, cols], F32, name="gate_" + name)
+                gate_tile = work.tile([P, cols], F32, name="gate_" + name)
                 done[name] = gate_tile[:]
             for name, position, func in GATES:
                 bias_column = position * HIDDEN_TILES + hidden_tile
@@ -181,71 +185,102 @@ def tile_lstmbaseline_pa_kernel(tc, x, W_ih0_words, W_ih0_scales, b_ih0, b_hh0, 
                     func=func,
                     bias=bias[:, bias_column : bias_column + 1],
                 )
-            nc.vector.tensor_tensor(
+            engine.tensor_tensor(
                 out=cell[:, offset : offset + cols], in0=done["i"], in1=done["g"], op=MULT
             )
 
-        def turn_round(values, blocks, name):
-            flipped = banks.tile([P, blocks, P], F32, tag="bank", name=name)
+        def turn_round(values, blocks, name, pool=banks, tag="bank"):
+            flipped = pool.tile([P, blocks, P], F32, tag=tag, name=name)
             for s in range(blocks):
                 nc.tensor.transpose(flipped[:, s, :], values[:, s * P : (s + 1) * P], identity[:])
             return flipped
 
-        def finish(unit, cell, gate_o):
+        def store(unit, hidden):
             hidden_tile, col0, cols = unit
-            blocks = cols // P
-            cell_turned = turn_round(cell, blocks, "cell_turned")
-            o_turned = turn_round(gate_o, blocks, "o_turned")
-            tanh_cell = work.tile([P, blocks, P], F32)
-            nc.scalar.activation(out=tanh_cell[:], in_=cell_turned[:], func=TANH)
-            hidden = work.tile([P, blocks, P], F32)
-            nc.vector.tensor_tensor(out=hidden[:], in0=tanh_cell[:], in1=o_turned[:], op=MULT)
             nc.sync.dma_start(
                 out=out_rows[
-                    :, col0 // P : col0 // P + blocks, hidden_tile * P : (hidden_tile + 1) * P
+                    :, col0 // P : (col0 + cols) // P, hidden_tile * P : (hidden_tile + 1) * P
                 ],
                 in_=hidden[:],
             )
 
-        def finish_on_vector(unit, cell, gate_o):
-            hidden_tile, col0, cols = unit
-            blocks = cols // P
+        def finish_turn(unit, cell, gate_o):
+            blocks = unit[2] // P
+            return turn_round(cell, blocks, "cell_turned"), turn_round(gate_o, blocks, "o_turned")
+
+        def finish_rest(unit, cell_turned, o_turned):
+            blocks = unit[2] // P
+            tanh_cell = work.tile([P, blocks, P], F32)
+            nc.scalar.activation(out=tanh_cell[:], in_=cell_turned[:], func=TANH)
+            hidden = leaving.tile([P, blocks, P], F32)
+            nc.vector.tensor_tensor(out=hidden[:], in0=tanh_cell[:], in1=o_turned[:], op=MULT)
+            store(unit, hidden)
+
+        def squares(engine, cell, gate_o):
+            c_squared = slow.tile([P, CHUNK], F32, name="c_squared")
+            c_times_o = slow.tile([P, CHUNK], F32, name="c_times_o")
+            calls = [
+                lambda: engine.tensor_tensor(out=c_squared[:], in0=cell[:], in1=cell[:], op=MULT),
+                lambda: engine.tensor_tensor(out=c_times_o[:], in0=cell[:], in1=gate_o[:], op=MULT),
+            ]
+            return c_squared, c_times_o, calls
+
+        def finish_on_vector(unit, c_squared, c_times_o):
             state = {}
+            halves = (slice(0, 2), slice(2, 4))
+            coefficients = [TANH_LEAD * tail for tail in TANH_TAIL] + [TANH_LEAD]
 
-            def square():
-                state["u"] = slow.tile([P, cols], F32, name="c_squared_%d" % hidden_tile)
-                state["t"] = state["u"]
-                nc.vector.tensor_tensor(out=state["u"][:], in0=cell[:], in1=cell[:], op=MULT)
+            def turn_u():
+                state["u"] = turn_round(c_squared, 4, "u_turned", held, "held")
 
-            def horner(coefficient, factor):
-                previous = state["t"]
-                state["t"] = slow.tile([P, cols], F32, name="horner_%d" % hidden_tile)
+            def turn_co():
+                state["co"] = turn_round(c_times_o, 4, "co_turned")
+
+            def first(half):
+                state[half] = slow.tile([P, 2, P], F32, name="horner_%d" % half)
+                nc.vector.tensor_scalar(
+                    out=state[half][:],
+                    in0=state["u"][:, halves[half], :],
+                    scalar1=coefficients[8],
+                    scalar2=coefficients[7],
+                    op0=MULT,
+                    op1=ADD,
+                )
+
+            def horner(half, coefficient):
+                previous = state[half]
+                state[half] = slow.tile([P, 2, P], F32, name="horner_%d" % half)
                 nc.vector.scalar_tensor_tensor(
-                    out=state["t"][:], in0=previous[:], scalar=coefficient, in1=factor[:], op0=ADD, op1=MULT
+                    out=state[half][:],
+                    in0=previous[:],
+                    scalar=coefficient,
+                    in1=state["u"][:, halves[half], :],
+                    op0=ADD,
+                    op1=MULT,
                 )
 
-            def times_o():
-                state["h"] = slow.tile([P, cols], F32, name="hidden_unturned")
+            def last(half):
+                if half == 0:
+                    state["h"] = leaving.tile([P, 4, P], F32, name="hidden")
                 nc.vector.scalar_tensor_tensor(
-                    out=state["h"][:], in0=state["t"][:], scalar=TANH_LEAD, in1=gate_o[:], op0=MULT, op1=MULT
+                    out=state["h"][:, halves[half], :],
+                    in0=state[half][:],
+                    scalar=coefficients[0],
+                    in1=state["co"][:, halves[half], :],
+                    op0=ADD,
+                    op1=MULT,
                 )
+                if half == 1:
+                    store(unit, state["h"])
 
-            def turn():
-                state["turned"] = turn_round(state["h"], blocks, "hidden_turned")
-
-            def leave():
-                hidden = slow.tile([P, blocks, P], F32, name="hidden_by_vector")
-                nc.vector.tensor_copy(out=hidden[:], in_=state["turned"][:])
-                nc.sync.dma_start(
-                    out=out_rows[
-                        :, col0 // P : col0 // P + blocks, hidden_tile * P : (hidden_tile + 1) * P
-                    ],
-                    in_=hidden[:],
-                )
-
-            steps = [square]
-            steps += [lambda k=k: horner(TANH_TAIL[k], state["u"]) for k in range(7, 0, -1)]
-            steps += [lambda: horner(TANH_TAIL[0], cell), times_o, lambda: None, turn, leave]
+            steps = [(0, turn_u)]
+            steps += [(1, lambda half=half: first(half)) for half in (0, 1)]
+            for k in (None, 6, 5, 4, 3, 2, 1):
+                if k == 2:
+                    steps += [(0, turn_co)]
+                added = 0.0 if k is None else coefficients[k]
+                steps += [(1, lambda half=half, added=added: horner(half, added)) for half in (0, 1)]
+            steps += [(1, lambda half=half: last(half)) for half in (0, 1)]
             return steps
 
         blocks = [(0, 0, CHUNK, (P, P, CHUNK // 2))]
@@ -254,7 +289,7 @@ def tile_lstmbaseline_pa_kernel(tc, x, W_ih0_words, W_ih0_scales, b_ih0, b_hh0, 
         blocks += [
             (HIDDEN_TILES - 1, col0, CHUNK // 2, (CHUNK // 2,)) for col0 in (CHUNK, CHUNK + CHUNK // 2)
         ]
-        later_x = {6: (4, 2), 7: (6, 2)}
+        later_x = 7
 
         first_turned = turn_x(0, 1)
         second_turned = turn_x(1, 1)
@@ -269,51 +304,65 @@ def tile_lstmbaseline_pa_kernel(tc, x, W_ih0_words, W_ih0_scales, b_ih0, b_hh0, 
         group_x(nc.vector.tensor_copy, 2, 2, third_turned)
         quantise_x(2, 2)
 
-        def advance(pending, moved):
-            if pending:
-                chain = pending[0]
-                pending.remove(chain)
-                chain[0]()
-                chain.remove(chain[0])
-                if chain:
-                    moved.append(chain)
-
         waiting = []
-        pending = []
-        moved = []
+        chains = []
+        steps = []
+        pool_calls = []
         index = 0
         for number, (hidden_tile, col0, cols, widths) in enumerate(blocks):
-            pool = slow if number in VECTOR_BLOCKS else work
-            cell = pool.tile([P, cols], F32, name="cell")
-            gate_o = pool.tile([P, cols], F32, name="gate_o")
+            block = (hidden_tile, col0, cols)
+            by_vector = number == 0 or number >= len(blocks) - LAST_ON_VECTOR
+            engine = nc.vector if by_vector else nc.gpsimd
+            cell = work.tile([P, cols], F32, name="cell")
+            gate_o = work.tile([P, cols], F32, name="gate_o")
             offset = 0
             for width in widths:
                 unit = (hidden_tile, col0 + offset, width)
                 gate_sums = matmuls(unit)
-                if index in later_x:
-                    pairs_turned = turn_x(*later_x[index])
-                activations(unit, gate_sums, pool, cell, gate_o, offset)
+                if index == later_x:
+                    turned_x = [turn_x(4, 2), turn_x(6, 2)]
+                activations(unit, gate_sums, engine, cell, gate_o, offset)
                 offset += width
-                if index in later_x:
-                    group_x(nc.vector.tensor_copy, *later_x[index], pairs_turned)
-                if index - 1 in later_x:
-                    quantise_x(*later_x[index - 1])
-                if index not in later_x and index - 1 not in later_x:
-                    advance(pending, moved)
+                if pool_calls:
+                    pool_calls[0]()
+                    pool_calls = pool_calls[1:]
                 if offset == cols:
                     if number in VECTOR_BLOCKS:
-                        pending.append(finish_on_vector((hidden_tile, col0, cols), cell, gate_o))
+                        c_squared, c_times_o, calls = squares(engine, cell, gate_o)
+                        if by_vector:
+                            calls[0]()
+                            calls[1]()
+                            chains.append((index + 2, finish_on_vector(block, c_squared, c_times_o)))
+                        else:
+                            pool_calls = pool_calls + calls
+                            chains.append((index + 3, finish_on_vector(block, c_squared, c_times_o)))
                     else:
-                        waiting.append(((hidden_tile, col0, cols), cell, gate_o))
+                        waiting.append((block, cell, gate_o))
+                turned = None
                 if len(waiting) > LAG:
-                    finish(*waiting[0])
+                    turned = finish_turn(*waiting[0])
+                budget = STEPS_PER_UNIT * width // CHUNK
+                if index == later_x:
+                    group_x(nc.vector.tensor_copy, 4, 2, turned_x[0])
+                    group_x(nc.vector.tensor_copy, 6, 2, turned_x[1])
+                    quantise_x(4, 2)
+                    quantise_x(6, 2)
+                    budget = 0
+                if not steps and budget and chains and chains[0][0] <= index:
+                    steps = chains[0][1]
+                    chains = chains[1:]
+                while steps and budget > 0:
+                    budget -= steps[0][0]
+                    steps[0][1]()
+                    steps = steps[1:]
+                if turned:
+                    finish_rest(waiting[0][0], *turned)
                     waiting = waiting[1:]
-                advance(pending, moved)
-                pending.extend(moved)
-                moved.clear()
                 index += 1
-        for chain in pending:
-            for step in chain:
-                step()
-        for block in waiting:
-            finish(*block)
+        for cost, call in steps:
+            call()
+        for first_unit, rest in chains:
+            for cost, call in rest:
+                call()
+        for block, cell, gate_o in waiting:
+            finish_rest(block, *finish_turn(block, cell, gate_o))

@@ -276,10 +276,9 @@ def tile_lstmbaseline_pa_kernel(tc, x, W_ih0_words, W_ih0_scales, b_ih0, b_hh0, 
             steps = [(0, turn_u)]
             steps += [(1, lambda half=half: first(half)) for half in (0, 1)]
             for k in (None, 6, 5, 4, 3, 2, 1):
-                if k == 2:
-                    steps += [(0, turn_co)]
                 added = 0.0 if k is None else coefficients[k]
                 steps += [(1, lambda half=half, added=added: horner(half, added)) for half in (0, 1)]
+            steps += [(0, turn_co)]
             steps += [(1, lambda half=half: last(half)) for half in (0, 1)]
             return steps
 
@@ -289,7 +288,7 @@ def tile_lstmbaseline_pa_kernel(tc, x, W_ih0_words, W_ih0_scales, b_ih0, b_hh0, 
         blocks += [
             (HIDDEN_TILES - 1, col0, CHUNK // 2, (CHUNK // 2,)) for col0 in (CHUNK, CHUNK + CHUNK // 2)
         ]
-        later_x = 7
+        later_x = {5: (4, 2), 6: (6, 2)}
 
         first_turned = turn_x(0, 1)
         second_turned = turn_x(1, 1)
@@ -319,8 +318,8 @@ def tile_lstmbaseline_pa_kernel(tc, x, W_ih0_words, W_ih0_scales, b_ih0, b_hh0, 
             for width in widths:
                 unit = (hidden_tile, col0 + offset, width)
                 gate_sums = matmuls(unit)
-                if index == later_x:
-                    turned_x = [turn_x(4, 2), turn_x(6, 2)]
+                if index in later_x:
+                    pairs_turned = turn_x(*later_x[index])
                 activations(unit, gate_sums, engine, cell, gate_o, offset)
                 offset += width
                 if pool_calls:
@@ -342,12 +341,12 @@ def tile_lstmbaseline_pa_kernel(tc, x, W_ih0_words, W_ih0_scales, b_ih0, b_hh0, 
                 if len(waiting) > LAG:
                     turned = finish_turn(*waiting[0])
                 budget = STEPS_PER_UNIT * width // CHUNK
-                if index == later_x:
-                    group_x(nc.vector.tensor_copy, 4, 2, turned_x[0])
-                    group_x(nc.vector.tensor_copy, 6, 2, turned_x[1])
-                    quantise_x(4, 2)
-                    quantise_x(6, 2)
-                    budget = 0
+                if index in later_x:
+                    group_x(nc.vector.tensor_copy, *later_x[index], pairs_turned)
+                    budget -= 2
+                if index - 1 in later_x:
+                    quantise_x(*later_x[index - 1])
+                    budget -= 1
                 if not steps and budget and chains and chains[0][0] <= index:
                     steps = chains[0][1]
                     chains = chains[1:]

@@ -37,8 +37,8 @@ TANH_TAIL = (
     25.354931336378282,
     -6.924973475538237,
 )
-VECTOR_BLOCKS = (0, 3, 6, 9)
-STEPS_PER_UNIT = 6
+VECTOR_BLOCKS = (0, 3, 6)
+STEPS_PER_UNIT = 5
 LAST_ON_VECTOR = 2
 WARM_UP_COLUMNS = 256
 WARM_UP_MATMULS = 9
@@ -225,7 +225,7 @@ def tile_lstmbaseline_pa_kernel(tc, x, W_ih0_words, W_ih0_scales, b_ih0, b_hh0, 
             ]
             return c_squared, c_times_o, calls
 
-        def finish_on_vector(unit, c_squared, c_times_o):
+        def finish_on_vector(unit, c_squared, c_times_o, clock):
             state = {}
             halves = (slice(0, 2), slice(2, 4))
             coefficients = [TANH_LEAD * tail for tail in TANH_TAIL] + [TANH_LEAD]
@@ -247,7 +247,9 @@ def tile_lstmbaseline_pa_kernel(tc, x, W_ih0_words, W_ih0_scales, b_ih0, b_hh0, 
                     op1=ADD,
                 )
 
-            def horner(half, coefficient):
+            def horner(half, coefficient, last_of_u):
+                if last_of_u:
+                    clock["free_from"] = clock["index"] + 1
                 previous = state[half]
                 state[half] = slow.tile([P, 2, P], F32, name="horner_%d" % half)
                 nc.vector.scalar_tensor_tensor(
@@ -277,7 +279,10 @@ def tile_lstmbaseline_pa_kernel(tc, x, W_ih0_words, W_ih0_scales, b_ih0, b_hh0, 
             steps += [(1, lambda half=half: first(half)) for half in (0, 1)]
             for k in (None, 6, 5, 4, 3, 2, 1):
                 added = 0.0 if k is None else coefficients[k]
-                steps += [(1, lambda half=half, added=added: horner(half, added)) for half in (0, 1)]
+                steps += [
+                    (1, lambda half=half, added=added, k=k: horner(half, added, k == 1 and half == 1))
+                    for half in (0, 1)
+                ]
             steps += [(0, turn_co)]
             steps += [(1, lambda half=half: last(half)) for half in (0, 1)]
             return steps
@@ -307,6 +312,7 @@ def tile_lstmbaseline_pa_kernel(tc, x, W_ih0_words, W_ih0_scales, b_ih0, b_hh0, 
         chains = []
         steps = []
         pool_calls = []
+        clock = {"index": 0, "free_from": 0}
         index = 0
         for number, (hidden_tile, col0, cols, widths) in enumerate(blocks):
             block = (hidden_tile, col0, cols)
@@ -331,10 +337,10 @@ def tile_lstmbaseline_pa_kernel(tc, x, W_ih0_words, W_ih0_scales, b_ih0, b_hh0, 
                         if by_vector:
                             calls[0]()
                             calls[1]()
-                            chains.append((index + 2, finish_on_vector(block, c_squared, c_times_o)))
+                            chains.append((index + 2, finish_on_vector(block, c_squared, c_times_o, clock)))
                         else:
                             pool_calls = pool_calls + calls
-                            chains.append((index + 3, finish_on_vector(block, c_squared, c_times_o)))
+                            chains.append((index + 3, finish_on_vector(block, c_squared, c_times_o, clock)))
                     else:
                         waiting.append((block, cell, gate_o))
                 turned = None
@@ -347,13 +353,17 @@ def tile_lstmbaseline_pa_kernel(tc, x, W_ih0_words, W_ih0_scales, b_ih0, b_hh0, 
                 if index - 1 in later_x:
                     quantise_x(*later_x[index - 1])
                     budget -= 1
-                if not steps and budget and chains and chains[0][0] <= index:
-                    steps = chains[0][1]
-                    chains = chains[1:]
-                while steps and budget > 0:
-                    budget -= steps[0][0]
-                    steps[0][1]()
-                    steps = steps[1:]
+                clock["index"] = index
+                while budget > 0:
+                    if not steps and chains and max(chains[0][0], clock["free_from"]) <= index:
+                        steps = chains[0][1]
+                        chains = chains[1:]
+                    if not steps:
+                        budget = 0
+                    else:
+                        budget -= steps[0][0]
+                        steps[0][1]()
+                        steps = steps[1:]
                 if turned:
                     finish_rest(waiting[0][0], *turned)
                     waiting = waiting[1:]

@@ -299,13 +299,15 @@ def tile_lstmbaseline_pa_kernel(tc, x, W_ih0_words, W_ih0_scales, b_ih0, b_hh0, 
         second_turned = turn_x(1, 1)
         bias_sum = banks.tile([P, 32], F32, tag="bank")
         nc.tensor.matmul(bias_sum[:], lhsT=bias_rows[:], rhs=pick[:], start=True, stop=True)
-        third_turned = turn_x(2, 2)
+        third_turned = turn_x(2, 1)
+        fourth_turned = turn_x(3, 1)
         group_x(nc.vector.tensor_copy, 0, 1, first_turned)
         group_x(nc.scalar.copy, 1, 1, second_turned)
+        group_x(nc.scalar.copy, 2, 1, third_turned)
+        group_x(nc.scalar.copy, 3, 1, fourth_turned)
         nc.vector.tensor_copy(out=bias[:], in_=bias_sum[:])
         quantise_x(0, 1)
         quantise_x(1, 1)
-        group_x(nc.vector.tensor_copy, 2, 2, third_turned)
         quantise_x(2, 2)
 
         waiting = []

@@ -23,7 +23,7 @@ PACK = 4
 
 ROWS_PER_PARTITION = B // P
 CHUNK = 512
-EARLY_TILES = 3
+EARLY_TILES = 2
 HIDDEN_TILES = H // P
 LAG = 2
 TANH_LEAD = 0.00012132876240913503

from contextlib import ExitStack

import concourse.mybir as mybir
from concourse.masks import make_identity

F32 = mybir.dt.float32
BF16 = mybir.dt.bfloat16
I32 = mybir.dt.int32
U32 = mybir.dt.uint32
U8 = mybir.dt.uint8
FP8X4 = mybir.dt.float8_e4m3fn_x4
FP4X4 = mybir.dt.float4_e2m1fn_x4
SIGMOID = mybir.ActivationFunctionType.Sigmoid
TANH = mybir.ActivationFunctionType.Tanh
ADD = mybir.AluOpType.add
MULT = mybir.AluOpType.mult

P = 128
B = 1024
K = 512
H = 1024
PACK = 4

ROWS_PER_PARTITION = B // P
CHUNK = 512
EARLY_TILES = 2
HIDDEN_TILES = H // P
LAG = 2
TANH_LEAD = 0.00012132876240913503
TANH_TAIL = (
    8242.068738109192,
    -2747.3558099211377,
    1098.930339531672,
    -444.67906624908534,
    179.53518132355708,
    -70.81795216358458,
    25.354931336378282,
    -6.924973475538237,
)
VECTOR_BLOCKS = (0, 3, 6)
STEPS_PER_UNIT = 5
LAST_ON_VECTOR = 2
WARM_UP_COLUMNS = 256
WARM_UP_MATMULS = 9

GATES = (("i", 0, SIGMOID), ("g", 2, TANH), ("o", 3, SIGMOID))

FLOPS = 2 * B * K * len(GATES) * H
BYTES = (
    B * K * 2
    + len(GATES) * H * (K // 2 + K // 32)
    + 2 * len(GATES) * H * 2
    + B * H * 4
)


def tile_lstmbaseline_pa_kernel(tc, x, W_ih0_words, W_ih0_scales, b_ih0, b_hh0, out):
    nc = tc.nc
    x_rows = x.rearrange("(p t) k -> p t k", t=ROWS_PER_PARTITION)
    out_rows = out.rearrange("(p t) n -> p t n", t=ROWS_PER_PARTITION)

    with ExitStack() as stack:
        keep = stack.enter_context(tc.tile_pool(name="keep", bufs=1))
        work = stack.enter_context(tc.tile_pool(name="work", bufs=LAG + 2))
        banks = stack.enter_context(tc.psum_pool(name="banks", bufs=7))
        held = stack.enter_context(tc.psum_pool(name="held", bufs=1))
        slow = stack.enter_context(tc.tile_pool(name="slow", bufs=2))
        leaving = stack.enter_context(tc.tile_pool(name="leaving", bufs=8))
        stack.enter_context(tc.manual_schedule())

        x_sb = keep.tile([P, ROWS_PER_PARTITION, K], BF16)
        words_early = keep.tile([P, 4, EARLY_TILES * 2 * P], U8, align_bytes=64)
        words_late = keep.tile([P, 4, (HIDDEN_TILES - EARLY_TILES) * 2 * P], U8, align_bytes=64)
        scales_early = keep.tile([P, 4, EARLY_TILES * P], U8, align_bytes=64)
        scales_late = keep.tile([P, 4, (HIDDEN_TILES - EARLY_TILES) * P], U8, align_bytes=64)
        bias_rows = keep.tile([P, P], BF16)
        words_hbm = W_ih0_words[0, :, :].bitcast(I32).rearrange("p (g c) -> p g c", g=4)
        scales_hbm = W_ih0_scales[0, :, :].bitcast(I32).rearrange("r (g c) -> r g c", g=4)
        early_words = EARLY_TILES * 2 * P // 4
        early_scales = EARLY_TILES * P // 4

        def load_x(engine, slot0, slot1):
            engine.dma_start(out=x_sb[:, slot0:slot1, :], in_=x_rows[:, slot0:slot1, :])

        def load_scales(scales_tile, c0, c1):
            nc.vector.memset(scales_tile[:].bitcast(I32), 0)
            for quadrant in range(4):
                nc.sync.dma_start(
                    out=scales_tile[32 * quadrant : 32 * quadrant + 4, :, :].bitcast(I32),
                    in_=scales_hbm[4 * quadrant : 4 * quadrant + 4, :, c0:c1],
                )

        zeros_words = keep.tile([P, WARM_UP_COLUMNS // 2], F32)
        nc.vector.memset(zeros_words[:], 0.0)
        zeros = zeros_words[:].bitcast(BF16)

        load_x(nc.sync, 0, 4)
        load_scales(scales_early, 0, early_scales)

        warm_in = keep.tile([P, 1], F32)
        warm_out = keep.tile([P, 1], F32)
        nc.vector.memset(warm_in[:], 0.0)
        nc.scalar.activation(out=warm_out[:], in_=warm_in[:], func=SIGMOID)

        nc.sync.dma_start(out=bias_rows[0:32, :], in_=b_ih0.rearrange("(r c) -> r c", c=P))
        nc.sync.dma_start(out=bias_rows[32:64, :], in_=b_hh0.rearrange("(r c) -> r c", c=P))
        nc.sync.dma_start(out=words_early[:].bitcast(I32), in_=words_hbm[:, :, 0:early_words])
        load_scales(scales_late, early_scales, H // 4)
        nc.sync.dma_start(out=words_late[:, 0, :].bitcast(I32), in_=words_hbm[:, 0, early_words:])
        nc.sync.dma_start(out=words_late[:, 2:4, :].bitcast(I32), in_=words_hbm[:, 2:4, early_words:])
        load_x(nc.sync, 4, 8)

        idle_sum = banks.tile([P, WARM_UP_COLUMNS], F32, tag="bank")
        for repeat in range(WARM_UP_MATMULS):
            nc.tensor.matmul(idle_sum[:], lhsT=zeros[:, 0:P], rhs=zeros, start=True, stop=True)

        identity = keep.tile([P, P], F32)
        make_identity(nc, identity[:])

        pick = keep.tile([P, 32], BF16)
        bias = keep.tile([P, 32], F32)
        nc.vector.memset(bias_rows[64:128, :], 0.0)
        nc.vector.tensor_tensor(out=pick[:], in0=identity[:, 0:32], in1=identity[:, 32:64], op=ADD)

        x_grouped = keep.tile([P, B, PACK], BF16, align_bytes=64)
        x_codes = keep.tile([P, B], U32, align_bytes=64)
        x_scales = keep.tile([P, B], U8, align_bytes=64)
        x_pairs = x_sb[:].bitcast(F32)

        def turn_x(slot0, slots):
            pairs_turned = banks.tile([P, slots, 2, P], F32, tag="bank")
            for s in range(slots):
                for u in range(2):
                    nc.tensor.transpose(
                        pairs_turned[:, s, u, :], x_pairs[:, slot0 + s, u : K // 2 : 2], identity[:]
                    )
            return pairs_turned

        def group_x(copy, slot0, slots, pairs_turned):
            cols = slice(slot0 * P, (slot0 + slots) * P)
            copy(
                out=x_grouped[:, cols, :].bitcast(F32).rearrange("p (s b) u -> p s b u", b=P),
                in_=pairs_turned[:].rearrange("p s u b -> p s b u"),
            )

        def quantise_x(slot0, slots):
            cols = slice(slot0 * P, (slot0 + slots) * P)
            nc.vector.quantize_mx(
                out=x_codes[:, cols].bitcast(FP8X4),
                scales=x_scales[:, cols],
                in_=x_grouped[:, cols, :].rearrange("p b t -> p (b t)"),
            )

        def matmuls(unit):
            hidden_tile, col0, cols = unit
            if hidden_tile < EARLY_TILES:
                words, scales, n0 = words_early, scales_early, hidden_tile * P
            else:
                words, scales, n0 = words_late, scales_late, (hidden_tile - EARLY_TILES) * P
            gate_sums = {}
            for name, position, func in GATES:
                gate_sums[name] = banks.tile([P, cols], F32, tag="bank", name="sum_" + name)
                nc.tensor.matmul_mx(
                    out=gate_sums[name][:],
                    lhsT=words[:, position, 2 * n0 : 2 * (n0 + P)].bitcast(FP4X4),
                    lhsT_scale=scales[:, position, n0 : n0 + P],
                    rhs=x_codes[:, col0 : col0 + cols].bitcast(FP8X4),
                    rhs_scale=x_scales[:, col0 : col0 + cols],
                    start=True,
                    stop=True,
                )
            return gate_sums

        def activations(unit, gate_sums, engine, cell, gate_o, offset):
            hidden_tile, col0, cols = unit
            done = {"o": gate_o[:, offset : offset + cols]}
            for name in ("i", "g"):
                gate_tile = work.tile([P, cols], F32, name="gate_" + name)
                done[name] = gate_tile[:]
            for name, position, func in GATES:
                bias_column = position * HIDDEN_TILES + hidden_tile
                nc.scalar.activation(
                    out=done[name],
                    in_=gate_sums[name][:],
                    func=func,
                    bias=bias[:, bias_column : bias_column + 1],
                )
            engine.tensor_tensor(
                out=cell[:, offset : offset + cols], in0=done["i"], in1=done["g"], op=MULT
            )

        def turn_round(values, blocks, name, pool=banks, tag="bank"):
            flipped = pool.tile([P, blocks, P], F32, tag=tag, name=name)
            for s in range(blocks):
                nc.tensor.transpose(flipped[:, s, :], values[:, s * P : (s + 1) * P], identity[:])
            return flipped

        def store(unit, hidden):
            hidden_tile, col0, cols = unit
            nc.sync.dma_start(
                out=out_rows[
                    :, col0 // P : (col0 + cols) // P, hidden_tile * P : (hidden_tile + 1) * P
                ],
                in_=hidden[:],
            )

        def finish_turn(unit, cell, gate_o):
            blocks = unit[2] // P
            return turn_round(cell, blocks, "cell_turned"), turn_round(gate_o, blocks, "o_turned")

        def finish_rest(unit, cell_turned, o_turned):
            blocks = unit[2] // P
            tanh_cell = work.tile([P, blocks, P], F32)
            nc.scalar.activation(out=tanh_cell[:], in_=cell_turned[:], func=TANH)
            hidden = leaving.tile([P, blocks, P], F32)
            nc.vector.tensor_tensor(out=hidden[:], in0=tanh_cell[:], in1=o_turned[:], op=MULT)
            store(unit, hidden)

        def squares(engine, cell, gate_o):
            c_squared = slow.tile([P, CHUNK], F32, name="c_squared")
            c_times_o = slow.tile([P, CHUNK], F32, name="c_times_o")
            calls = [
                lambda: engine.tensor_tensor(out=c_squared[:], in0=cell[:], in1=cell[:], op=MULT),
                lambda: engine.tensor_tensor(out=c_times_o[:], in0=cell[:], in1=gate_o[:], op=MULT),
            ]
            return c_squared, c_times_o, calls

        def finish_on_vector(unit, c_squared, c_times_o, clock):
            state = {}
            halves = (slice(0, 2), slice(2, 4))
            coefficients = [TANH_LEAD * tail for tail in TANH_TAIL] + [TANH_LEAD]

            def turn_u():
                state["u"] = turn_round(c_squared, 4, "u_turned", held, "held")

            def turn_co():
                state["co"] = turn_round(c_times_o, 4, "co_turned")

            def first(half):
                state[half] = slow.tile([P, 2, P], F32, name="horner_%d" % half)
                nc.vector.tensor_scalar(
                    out=state[half][:],
                    in0=state["u"][:, halves[half], :],
                    scalar1=coefficients[8],
                    scalar2=coefficients[7],
                    op0=MULT,
                    op1=ADD,
                )

            def horner(half, coefficient, last_of_u):
                if last_of_u:
                    clock["free_from"] = clock["index"] + 1
                previous = state[half]
                state[half] = slow.tile([P, 2, P], F32, name="horner_%d" % half)
                nc.vector.scalar_tensor_tensor(
                    out=state[half][:],
                    in0=previous[:],
                    scalar=coefficient,
                    in1=state["u"][:, halves[half], :],
                    op0=ADD,
                    op1=MULT,
                )

            def last(half):
                if half == 0:
                    state["h"] = leaving.tile([P, 4, P], F32, name="hidden")
                nc.vector.scalar_tensor_tensor(
                    out=state["h"][:, halves[half], :],
                    in0=state[half][:],
                    scalar=coefficients[0],
                    in1=state["co"][:, halves[half], :],
                    op0=ADD,
                    op1=MULT,
                )
                if half == 1:
                    store(unit, state["h"])

            steps = [(0, turn_u)]
            steps += [(1, lambda half=half: first(half)) for half in (0, 1)]
            for k in (None, 6, 5, 4, 3, 2, 1):
                added = 0.0 if k is None else coefficients[k]
                steps += [
                    (1, lambda half=half, added=added, k=k: horner(half, added, k == 1 and half == 1))
                    for half in (0, 1)
                ]
            steps += [(0, turn_co)]
            steps += [(1, lambda half=half: last(half)) for half in (0, 1)]
            return steps

        blocks = [(0, 0, CHUNK, (P, P, CHUNK // 2))]
        blocks += [(hidden_tile, 0, CHUNK, (CHUNK,)) for hidden_tile in range(1, HIDDEN_TILES)]
        blocks += [(hidden_tile, CHUNK, CHUNK, (CHUNK,)) for hidden_tile in range(HIDDEN_TILES - 1)]
        blocks += [
            (HIDDEN_TILES - 1, col0, CHUNK // 2, (CHUNK // 2,)) for col0 in (CHUNK, CHUNK + CHUNK // 2)
        ]
        later_x = {5: (4, 2), 6: (6, 2)}

        first_turned = turn_x(0, 1)
        second_turned = turn_x(1, 1)
        bias_sum = banks.tile([P, 32], F32, tag="bank")
        nc.tensor.matmul(bias_sum[:], lhsT=bias_rows[:], rhs=pick[:], start=True, stop=True)
        third_turned = turn_x(2, 1)
        fourth_turned = turn_x(3, 1)
        group_x(nc.vector.tensor_copy, 0, 1, first_turned)
        group_x(nc.scalar.copy, 1, 1, second_turned)
        group_x(nc.scalar.copy, 2, 1, third_turned)
        group_x(nc.scalar.copy, 3, 1, fourth_turned)
        nc.vector.tensor_copy(out=bias[:], in_=bias_sum[:])
        quantise_x(0, 1)
        quantise_x(1, 1)
        quantise_x(2, 2)

        waiting = []
        chains = []
        steps = []
        pool_calls = []
        clock = {"index": 0, "free_from": 0}
        index = 0
        for number, (hidden_tile, col0, cols, widths) in enumerate(blocks):
            block = (hidden_tile, col0, cols)
            by_vector = number == 0 or number >= len(blocks) - LAST_ON_VECTOR
            engine = nc.vector if by_vector else nc.gpsimd
            cell = work.tile([P, cols], F32, name="cell")
            gate_o = work.tile([P, cols], F32, name="gate_o")
            offset = 0
            for width in widths:
                unit = (hidden_tile, col0 + offset, width)
                gate_sums = matmuls(unit)
                if index in later_x:
                    pairs_turned = turn_x(*later_x[index])
                activations(unit, gate_sums, engine, cell, gate_o, offset)
                offset += width
                if pool_calls:
                    pool_calls[0]()
                    pool_calls = pool_calls[1:]
                if offset == cols:
                    if number in VECTOR_BLOCKS:
                        c_squared, c_times_o, calls = squares(engine, cell, gate_o)
                        if by_vector:
                            calls[0]()
                            calls[1]()
                            chains.append((index + 2, finish_on_vector(block, c_squared, c_times_o, clock)))
                        else:
                            pool_calls = pool_calls + calls
                            chains.append((index + 3, finish_on_vector(block, c_squared, c_times_o, clock)))
                    else:
                        waiting.append((block, cell, gate_o))
                turned = None
                if len(waiting) > LAG:
                    turned = finish_turn(*waiting[0])
                budget = STEPS_PER_UNIT * width // CHUNK
                if index in later_x:
                    group_x(nc.vector.tensor_copy, *later_x[index], pairs_turned)
                    budget -= 2
                if index - 1 in later_x:
                    quantise_x(*later_x[index - 1])
                    budget -= 1
                clock["index"] = index
                while budget > 0:
                    if not steps and chains and max(chains[0][0], clock["free_from"]) <= index:
                        steps = chains[0][1]
                        chains = chains[1:]
                    if not steps:
                        budget = 0
                    else:
                        budget -= steps[0][0]
                        steps[0][1]()
                        steps = steps[1:]
                if turned:
                    finish_rest(waiting[0][0], *turned)
                    waiting = waiting[1:]
                index += 1
        for cost, call in steps:
            call()
        for first_unit, rest in chains:
            for cost, call in rest:
                call()
        for block, cell, gate_o in waiting:
            finish_rest(block, *finish_turn(block, cell, gate_o))
